import numpy as np
import ml_dtypes


def mxq(x, axis, fmt="e4m3"):
    dtype, down = {"e4m3": (ml_dtypes.float8_e4m3fn, 7), "e5m2": (ml_dtypes.float8_e5m2, 14)}[fmt]
    v = np.moveaxis(np.asarray(x, np.float32).astype(ml_dtypes.bfloat16).astype(np.float64), axis, -1)
    blocks = v.reshape(v.shape[:-1] + (-1, 32))
    amax = np.abs(blocks).max(-1, keepdims=True)
    byte = np.maximum(np.where(amax > 0, np.frexp(amax)[1] - 1 + 127, 0) - down, 1)
    scale = np.exp2(byte - 127.0)
    codes = (blocks / scale).astype(np.float32).astype(dtype).astype(np.float64)
    return np.moveaxis((codes * scale).reshape(v.shape), -1, axis)


WIDE = False


def mx_kscale(k):
    if not WIDE:
        return np.ones(k)
    levels = np.array([10, -10, 5, -5, 0])
    a = np.random.permutation(np.resize(levels, k // 512 * 4)).reshape(k // 512, 4)
    idx = np.arange(k)
    return np.exp2(a[idx // 512, idx % 128 // 32])


BF16 = ml_dtypes.bfloat16


def bf(x):
    return np.asarray(x, np.float32).astype(BF16)


def f64(x):
    return np.asarray(x).astype(np.float64)


E2M1 = np.array([0.0, 0.5, 1.0, 1.5, 2.0, 3.0, 4.0, 6.0, -0.0, -0.5, -1.0, -1.5, -2.0, -3.0, -4.0, -6.0])


def pack_weight(w, fmt):
    k, n = w.shape
    w = f64(bf(w)).reshape(k // 32, 32, n)
    amax = np.abs(w).max(1)
    if fmt == "e4m3":
        byte = np.frexp(amax)[1] - 1 + 127 - 7
    else:
        mant, ex = np.frexp(amax / 6.0)
        byte = np.where(mant > 0.5, ex, ex - 1) + 127
    byte = np.clip(np.where(amax > 0, byte, 1), 1, 254)
    scaled = (w * np.exp2(127.0 - byte)[:, None, :]).reshape(k, n).astype(np.float32)
    by_word = np.ascontiguousarray(scaled.reshape(k // 512, 128, 4, n).transpose(0, 1, 3, 2))
    if fmt == "e4m3":
        words = by_word.astype(ml_dtypes.float8_e4m3fn).view(np.uint8)
    else:
        c = by_word.astype(ml_dtypes.float4_e2m1fn).view(np.uint8) & 0xF
        words = c[..., 0::2] | (c[..., 1::2] << 4)
    return np.ascontiguousarray(words), np.ascontiguousarray(byte.astype(np.uint8).reshape(k // 512, 16, n))


def unpack_weight(words, scales, fmt):
    g, p, n, _ = words.shape
    if fmt == "e4m3":
        vals = np.ascontiguousarray(words).view(ml_dtypes.float8_e4m3fn).astype(np.float64)
    else:
        nib = np.empty((g, p, n, 4), np.uint8)
        nib[..., 0::2] = words & 0xF
        nib[..., 1::2] = words >> 4
        vals = E2M1[nib]
    vals = vals * np.repeat(np.exp2(scales.astype(np.float64) - 127.0), 8, axis=1)[..., None]
    return vals.transpose(0, 1, 3, 2).reshape(g * 512, n)


N, H, S, R, T = 4096, 512, 4, 128, 128


def sigmoid(v):
    return 1.0 / (1.0 + np.exp(-v))


def setup_inputs():
    s, t = mx_kscale(H), mx_kscale(H)
    g = np.exp(np.random.standard_normal((S, N)))
    encodings = bf(np.random.standard_normal((N, H)) * s)
    alphas = bf(g / g.sum(axis=0, keepdims=True))
    W1 = np.random.standard_normal((S, H, H)) * 1.4 / np.sqrt(H) / s[None, :, None] * t[None, None, :]
    b1 = bf(np.random.standard_normal((S, H)) * 0.3 * t[None, :])
    W2 = np.random.standard_normal((S, H, T)) * 2.0 / np.sqrt(H) / t[None, :, None]
    b2 = bf(np.random.standard_normal((S, T)) * 0.5)
    W1_words, W1_scales = pack_weight(W1.reshape(-1, H), "e4m3")
    W2_words, W2_scales = pack_weight(W2.reshape(-1, T), "e4m3")
    return {"encodings": encodings,
            "alphas": alphas,
            "W1_words": W1_words,
            "W1_scales": W1_scales,
            "b1": b1,
            "W2_words": W2_words,
            "W2_scales": W2_scales,
            "b2": b2}


def reference(encodings, alphas, W1_words, W1_scales, b1, W2_words, W2_scales, b2):
    h0 = np.maximum(f64(encodings), 0.0)
    h1 = np.maximum((mxq(h0, 1, "e4m3") @ unpack_weight(W1_words, W1_scales, "e4m3").reshape(S, H, H)) + f64(b1)[:, None, :], 0.0)
    out = sigmoid((mxq(h1, 2, "e4m3") @ unpack_weight(W2_words, W2_scales, "e4m3").reshape(S, H, T)) + f64(b2)[:, None, :])
    return np.sum(f64(alphas)[:, :, None] * out, axis=0)

@@ -1,0 +1,313 @@
+from contextlib import ExitStack
+
+import concourse.mybir as mybir
+from concourse.masks import make_identity
+
+F32 = mybir.dt.float32
+BF16 = mybir.dt.bfloat16
+I32 = mybir.dt.int32
+U8 = mybir.dt.uint8
+FP8X4 = mybir.dt.float8_e4m3fn_x4
+ACT = mybir.ActivationFunctionType
+ALU = mybir.AluOpType
+
+P = 128
+PACK = 4
+N_TOKENS = 4096
+H = 512
+S = 4
+T = 128
+CHUNK = 512
+TILES = CHUNK // P
+N_CHUNKS = N_TOKENS // CHUNK
+N_TILES = N_TOKENS // P
+H_TILES = H // P
+STEPS = N_CHUNKS * S
+
+REGROUP_LAG = 3
+QUANTISE_LAG = REGROUP_LAG + 1
+LAYER2_LAG = QUANTISE_LAG + 1
+TRANSPOSE_LAG = LAYER2_LAG + S
+WEIGH_LAG = TRANSPOSE_LAG + 1
+STORE_LAG = WEIGH_LAG + 1
+H0_QUANTISE_LEAD = 1
+H0_COPY_LEAD = (4, 2)
+H0_TRANSPOSE_LEAD = (5, 3)
+H0_RELU_LEAD = 6
+LOAD_LEAD = 12
+
+FLOPS = 2 * S * N_TOKENS * H * (H + T)
+
+
+def tile_moe_pb_e_kernel(
+    tc, encodings, alphas, W1_words, W1_scales, b1, W2_words, W2_scales, b2, out
+):
+    nc = tc.nc
+    enc_chunks = encodings.rearrange("(c i p) h -> c p i h", i=TILES, p=P)
+    out_tiles = out.rearrange("(j p) t -> j p t", p=P)
+
+    with ExitStack() as ctx:
+        ctx.enter_context(tc.manual_schedule())
+        const = ctx.enter_context(tc.tile_pool(name="const", bufs=1))
+        enc_pool = ctx.enter_context(tc.tile_pool(name="enc", bufs=4))
+        h0_pool = ctx.enter_context(tc.tile_pool(name="h0", bufs=2))
+        y_pool = ctx.enter_context(tc.tile_pool(name="y", bufs=2 * H_TILES))
+        planes_pool = ctx.enter_context(tc.tile_pool(name="planes", bufs=REGROUP_LAG + 2))
+        h1_pool = ctx.enter_context(tc.tile_pool(name="h1", bufs=3))
+        prob_pool = ctx.enter_context(tc.tile_pool(name="prob", bufs=2 * S))
+        res_pool = ctx.enter_context(tc.tile_pool(name="res", bufs=4))
+        psum_x = ctx.enter_context(tc.psum_pool(name="psum_x", bufs=4))
+        psum_e = ctx.enter_context(tc.psum_pool(name="psum_e", bufs=1))
+        psum_z = ctx.enter_context(tc.psum_pool(name="psum_z", bufs=1))
+        psum_f = ctx.enter_context(tc.psum_pool(name="psum_f", bufs=2))
+
+        def load_chunk(c):
+            enc_sb = enc_pool.tile([P, TILES, H], BF16, name="enc_sb")
+            nc.sync.dma_start(out=enc_sb[:], in_=enc_chunks[c])
+            return enc_sb
+
+        rows = const.tile([P, H + T], BF16, name="rows")
+        nc.vector.memset(rows[:], 0.0)
+        w1_planes_in = const.tile([P, H], U8, name="w1_planes_in", align_bytes=64)
+        w2_planes = const.tile([P, T], U8, name="w2_planes", align_bytes=64)
+        nc.vector.memset(w1_planes_in[:].bitcast(I32), 0)
+        nc.vector.memset(w2_planes[:].bitcast(I32), 0)
+        identity = const.tile([P, P], F32, name="identity")
+        make_identity(nc, identity[:])
+
+        nc.sync.dma_start(out=rows[0:S, 0:H], in_=b1)
+        nc.sync.dma_start(out=rows[0:S, H : H + T], in_=b2)
+        enc_tiles = {0: load_chunk(0)}
+        for quadrant in range(4):
+            nc.sync.dma_start(
+                out=w1_planes_in[32 * quadrant : 32 * quadrant + 16, :].bitcast(I32),
+                in_=W1_scales[:, 4 * quadrant : 4 * quadrant + 4, :].bitcast(I32),
+            )
+        w1_in = const.tile([P, S, H], I32, name="w1_in", align_bytes=64)
+        for s in range(S):
+            nc.sync.dma_start(
+                out=w1_in[:, s, :],
+                in_=W1_words[s].rearrange("p n t -> p (n t)").bitcast(I32),
+            )
+        alpha_rows = const.tile([P, P], BF16, name="alpha_rows")
+        nc.sync.dma_start(out=alpha_rows[:], in_=alphas.rearrange("s (j p) -> (s j) p", p=P))
+        for quadrant in range(4):
+            nc.sync.dma_start(
+                out=w2_planes[32 * quadrant : 32 * quadrant + 16, :].bitcast(I32),
+                in_=W2_scales[:, 4 * quadrant : 4 * quadrant + 4, :].bitcast(I32),
+            )
+        w2_words = const.tile([P, S, T], I32, name="w2_words", align_bytes=64)
+        nc.sync.dma_start(
+            out=w2_words[:], in_=W2_words.rearrange("g p n t -> p g (n t)").bitcast(I32)
+        )
+        enc_tiles[1] = load_chunk(1)
+        enc_tiles[2] = load_chunk(2)
+
+        rows_f32 = const.tile([P, H_TILES + 1, P], F32, name="rows_f32")
+        nc.vector.tensor_copy(
+            out=rows_f32[:, 0:H_TILES, :].rearrange("p tau (a i) -> p tau a i", i=PACK),
+            in_=rows[:, 0:H].rearrange("p (a tau i) -> p tau a i", tau=H_TILES, i=PACK),
+        )
+        nc.vector.tensor_copy(out=rows_f32[:, H_TILES, :], in_=rows[:, H : H + T])
+        b1_ps = psum_f.tile([P, H_TILES, P], F32, name="f_ps")
+        for tau in range(H_TILES):
+            nc.tensor.transpose(b1_ps[:, tau, :], rows_f32[:, tau, :], identity[:])
+        b2_ps = psum_f.tile([P, H_TILES, P], F32, name="f_ps")
+        nc.tensor.transpose(b2_ps[:, 0, :], rows_f32[:, H_TILES, :], identity[:])
+        b1_cols = const.tile([P, H_TILES, S], F32, name="b1_cols")
+        nc.vector.tensor_copy(out=b1_cols[:], in_=b1_ps[:, :, 0:S])
+        b2_cols = const.tile([P, S], F32, name="b2_cols")
+        nc.vector.tensor_copy(out=b2_cols[:], in_=b2_ps[:, 0, 0:S])
+
+        h0_tiles = {}
+        h0_grouped_tiles = {}
+        e_ps_tiles = {}
+        h0_operands = {}
+        planes_tiles = {}
+        h1_grouped_tiles = {}
+        h1_operands = {}
+        prob_tiles = {}
+        f_ps_tiles = {}
+        res_tiles = {}
+
+        def relu_h0(c):
+            h0_tiles[c] = h0_pool.tile([P, TILES, H], BF16, name="h0")
+            nc.vector.tensor_scalar_max(out=h0_tiles[c][:], in0=enc_tiles[c][:], scalar1=0.0)
+            h0_grouped_tiles[c] = h0_pool.tile(
+                [P, CHUNK * PACK], BF16, name="h0_grouped", align_bytes=64
+            )
+
+        def transpose_h0(c, half):
+            e_ps = psum_e.tile([P, 2, 2, P], F32, name="e_ps")
+            for i in range(2):
+                words = h0_tiles[c][:, 2 * half + i, :].bitcast(F32)
+                for u in range(2):
+                    nc.tensor.transpose(e_ps[:, i, u, :], words[:, u : H // 2 : 2], identity[:])
+            e_ps_tiles[c, half] = e_ps
+
+        def copy_h0(c, half):
+            grouped_words = h0_grouped_tiles[c][:].bitcast(F32).rearrange(
+                "p (i n u) -> p i n u", i=TILES, u=2
+            )
+            nc.vector.tensor_copy(
+                out=grouped_words[:, 2 * half : 2 * half + 2, :, :],
+                in_=e_ps_tiles[c, half][:].rearrange("p i u n -> p i n u"),
+            )
+
+        def quantise_h0(c):
+            h0_codes = h0_pool.tile([P, CHUNK], I32, name="h0_codes", align_bytes=64)
+            h0_plane = h0_pool.tile([P, CHUNK], U8, name="h0_plane", align_bytes=64)
+            nc.vector.quantize_mx(
+                out=h0_codes[:].bitcast(FP8X4), scales=h0_plane[:], in_=h0_grouped_tiles[c][:]
+            )
+            h0_operands[c] = (h0_codes, h0_plane)
+
+        def layer1(k):
+            c, s = divmod(k, S)
+            h0_codes, h0_plane = h0_operands[c]
+            planes = planes_pool.tile([P, PACK, CHUNK], BF16, name="planes")
+            for tau in range(H_TILES):
+                x_ps = psum_x.tile([P, CHUNK], F32, name="x_ps")
+                nc.tensor.matmul_mx(
+                    out=x_ps[:],
+                    lhsT=w1_tiles[:, s, tau, :].bitcast(FP8X4),
+                    lhsT_scale=w1_planes[4 * s : P, tau, :],
+                    rhs=h0_codes[:].bitcast(FP8X4),
+                    rhs_scale=h0_plane[:],
+                    start=True,
+                    stop=True,
+                )
+                y = y_pool.tile([P, CHUNK], BF16, name="y")
+                nc.scalar.activation(
+                    out=y[:], in_=x_ps[:], func=ACT.Relu, bias=b1_cols[:, tau, s : s + 1], scale=1.0
+                )
+                nc.sync.dma_start(out=planes[tau:P:H_TILES, :, :], in_=y[:])
+            planes_tiles[k] = planes
+
+        def regroup_h1(k):
+            h1_grouped = h1_pool.tile([P, CHUNK * PACK], BF16, name="h1_grouped", align_bytes=64)
+            nc.vector.tensor_copy(
+                out=h1_grouped[:].rearrange("p (c i t) -> p c t i", i=4, t=PACK),
+                in_=planes_tiles[k][:].rearrange("p t (c i) -> p c t i", i=4),
+            )
+            h1_grouped_tiles[k] = h1_grouped
+
+        def quantise_h1(k):
+            h1_codes = h1_pool.tile([P, CHUNK], I32, name="h1_codes", align_bytes=64)
+            h1_plane = h1_pool.tile([P, CHUNK], U8, name="h1_plane", align_bytes=64)
+            nc.vector.quantize_mx(
+                out=h1_codes[:].bitcast(FP8X4), scales=h1_plane[:], in_=h1_grouped_tiles[k][:]
+            )
+            h1_operands[k] = (h1_codes, h1_plane)
+
+        def layer2(k):
+            s = k % S
+            h1_codes, h1_plane = h1_operands[k]
+            z_ps = psum_z.tile([P, CHUNK], F32, name="z_ps")
+            nc.tensor.matmul_mx(
+                out=z_ps[:],
+                lhsT=w2_words[:, s, :].bitcast(FP8X4),
+                lhsT_scale=w2_planes[4 * s : P, :],
+                rhs=h1_codes[:].bitcast(FP8X4),
+                rhs_scale=h1_plane[:],
+                start=True,
+                stop=True,
+            )
+            prob = prob_pool.tile([P, CHUNK], F32, name="prob")
+            nc.scalar.activation(
+                out=prob[:], in_=z_ps[:], func=ACT.Sigmoid, bias=b2_cols[:, s : s + 1], scale=1.0
+            )
+            prob_tiles[k] = prob
+
+        def transpose_probs(j):
+            c, i = divmod(j, TILES)
+            f_ps = psum_f.tile([P, S, T], F32, name="f_ps")
+            for s in range(S):
+                nc.tensor.transpose(
+                    f_ps[:, s, :], prob_tiles[c * S + s][:, i * P : (i + 1) * P], identity[:]
+                )
+            f_ps_tiles[j] = f_ps
+
+        def weigh(j):
+            f_ps = f_ps_tiles[j]
+            res = res_pool.tile([P, T], F32, name="res")
+            nc.vector.tensor_scalar(
+                out=res[:],
+                in0=f_ps[:, 0, :],
+                scalar1=alpha_cols[:, 0, j : j + 1],
+                scalar2=None,
+                op0=ALU.mult,
+            )
+            for s in range(1, S):
+                nc.vector.scalar_tensor_tensor(
+                    out=res[:],
+                    in0=f_ps[:, s, :],
+                    scalar=alpha_cols[:, s, j : j + 1],
+                    in1=res[:],
+                    op0=ALU.mult,
+                    op1=ALU.add,
+                )
+            res_tiles[j] = res
+
+        def chunk_due(k, lead):
+            c, s = divmod(k + lead, S)
+            return c if s == 0 and 0 <= c < N_CHUNKS else None
+
+        def step(k):
+            c = chunk_due(k, LOAD_LEAD)
+            if c is not None and c not in enc_tiles:
+                enc_tiles[c] = load_chunk(c)
+            if 0 <= k < STEPS:
+                layer1(k)
+            if 0 <= k - LAYER2_LAG < STEPS:
+                layer2(k - LAYER2_LAG)
+            if 0 <= k - QUANTISE_LAG < STEPS:
+                quantise_h1(k - QUANTISE_LAG)
+            if 0 <= k - REGROUP_LAG < STEPS:
+                regroup_h1(k - REGROUP_LAG)
+            if 0 <= k - TRANSPOSE_LAG < N_TILES:
+                transpose_probs(k - TRANSPOSE_LAG)
+            if 0 <= k - WEIGH_LAG < N_TILES:
+                weigh(k - WEIGH_LAG)
+            if 0 <= k - STORE_LAG < N_TILES:
+                nc.sync.dma_start(out=out_tiles[k - STORE_LAG], in_=res_tiles[k - STORE_LAG][:])
+            c = chunk_due(k, H0_RELU_LEAD)
+            if c is not None:
+                relu_h0(c)
+            for half in range(2):
+                c = chunk_due(k, H0_TRANSPOSE_LEAD[half])
+                if c is not None:
+                    transpose_h0(c, half)
+                c = chunk_due(k, H0_COPY_LEAD[half])
+                if c is not None:
+                    copy_h0(c, half)
+            c = chunk_due(k, H0_QUANTISE_LEAD)
+            if c is not None:
+                quantise_h0(c)
+
+        for k in range(-H0_RELU_LEAD, 0):
+            step(k)
+
+        w1_planes = const.tile([P, H_TILES, P], U8, name="w1_planes", align_bytes=64)
+        nc.vector.tensor_copy(
+            out=w1_planes[:].bitcast(I32),
+            in_=w1_planes_in[:].bitcast(I32).rearrange("p (a tau) -> p tau a", tau=H_TILES),
+        )
+        w1_tiles = const.tile([P, S, H_TILES, P], I32, name="w1_tiles", align_bytes=64)
+        for s in range(S):
+            nc.vector.tensor_copy(
+                out=w1_tiles[:, s, :, :].rearrange("p tau (a i) -> p tau a i", i=PACK),
+                in_=w1_in[:, s, :].rearrange("p (a tau i) -> p tau a i", tau=H_TILES, i=PACK),
+            )
+
+        alpha_f32 = const.tile([P, P], F32, name="alpha_f32")
+        nc.vector.tensor_copy(out=alpha_f32[:], in_=alpha_rows[:])
+        alpha_ps = psum_f.tile([P, H_TILES, P], F32, name="f_ps")
+        nc.tensor.transpose(alpha_ps[:, 0, :], alpha_f32[:], identity[:])
+        alpha_cols = const.tile([P, S, N_TILES], F32, name="alpha_cols")
+        nc.vector.tensor_copy(
+            out=alpha_cols[:].rearrange("p s j -> p (s j)"), in_=alpha_ps[:, 0, :]
+        )
+
+        for k in range(STEPS + STORE_LAG):
+            step(k)

@@ -27,7 +27,7 @@ STEPS = N_CHUNKS * S
 REGROUP_LAG = 3
 QUANTISE_LAG = REGROUP_LAG + 1
 LAYER2_LAG = QUANTISE_LAG + 1
-TRANSPOSE_LAG = LAYER2_LAG + S
+TRANSPOSE_LAG = LAYER2_LAG + 1
 WEIGH_LAG = TRANSPOSE_LAG + 1
 STORE_LAG = WEIGH_LAG + 1
 H0_QUANTISE_LEAD = 1
@@ -44,7 +44,7 @@ def tile_moe_pb_e_kernel(
 ):
     nc = tc.nc
     enc_chunks = encodings.rearrange("(c i p) h -> c p i h", i=TILES, p=P)
-    out_tiles = out.rearrange("(j p) t -> j p t", p=P)
+    out_chunks = out.rearrange("(c i p) t -> c p i t", i=TILES, p=P)
 
     with ExitStack() as ctx:
         ctx.enter_context(tc.manual_schedule())
@@ -54,8 +54,8 @@ def tile_moe_pb_e_kernel(
         y_pool = ctx.enter_context(tc.tile_pool(name="y", bufs=2 * H_TILES))
         planes_pool = ctx.enter_context(tc.tile_pool(name="planes", bufs=REGROUP_LAG + 2))
         h1_pool = ctx.enter_context(tc.tile_pool(name="h1", bufs=3))
-        prob_pool = ctx.enter_context(tc.tile_pool(name="prob", bufs=2 * S))
-        res_pool = ctx.enter_context(tc.tile_pool(name="res", bufs=4))
+        prob_pool = ctx.enter_context(tc.tile_pool(name="prob", bufs=3))
+        res_pool = ctx.enter_context(tc.tile_pool(name="res", bufs=2))
         psum_x = ctx.enter_context(tc.psum_pool(name="psum_x", bufs=4))
         psum_e = ctx.enter_context(tc.psum_pool(name="psum_e", bufs=1))
         psum_z = ctx.enter_context(tc.psum_pool(name="psum_z", bufs=1))
@@ -75,9 +75,9 @@ def tile_moe_pb_e_kernel(
         identity = const.tile([P, P], F32, name="identity")
         make_identity(nc, identity[:])
 
+        enc_tiles = {0: load_chunk(0)}
         nc.sync.dma_start(out=rows[0:S, 0:H], in_=b1)
         nc.sync.dma_start(out=rows[0:S, H : H + T], in_=b2)
-        enc_tiles = {0: load_chunk(0)}
         for quadrant in range(4):
             nc.sync.dma_start(
                 out=w1_planes_in[32 * quadrant : 32 * quadrant + 16, :].bitcast(I32),
@@ -219,35 +219,32 @@ def tile_moe_pb_e_kernel(
             )
             prob_tiles[k] = prob
 
-        def transpose_probs(j):
-            c, i = divmod(j, TILES)
-            f_ps = psum_f.tile([P, S, T], F32, name="f_ps")
-            for s in range(S):
-                nc.tensor.transpose(
-                    f_ps[:, s, :], prob_tiles[c * S + s][:, i * P : (i + 1) * P], identity[:]
-                )
-            f_ps_tiles[j] = f_ps
+        def transpose_probs(k):
+            f_ps = psum_f.tile([P, TILES, T], F32, name="f_ps")
+            for i in range(TILES):
+                nc.tensor.transpose(f_ps[:, i, :], prob_tiles[k][:, i * P : (i + 1) * P], identity[:])
+            f_ps_tiles[k] = f_ps
 
-        def weigh(j):
-            f_ps = f_ps_tiles[j]
-            res = res_pool.tile([P, T], F32, name="res")
-            nc.vector.tensor_scalar(
-                out=res[:],
-                in0=f_ps[:, 0, :],
-                scalar1=alpha_cols[:, 0, j : j + 1],
-                scalar2=None,
-                op0=ALU.mult,
-            )
-            for s in range(1, S):
-                nc.vector.scalar_tensor_tensor(
-                    out=res[:],
-                    in0=f_ps[:, s, :],
-                    scalar=alpha_cols[:, s, j : j + 1],
-                    in1=res[:],
-                    op0=ALU.mult,
-                    op1=ALU.add,
-                )
-            res_tiles[j] = res
+        def weigh(k):
+            c, s = divmod(k, S)
+            if s == 0:
+                res_tiles[c] = res_pool.tile([P, TILES, T], F32, name="res")
+            for i in range(TILES):
+                weight = alpha_cols[:, s, c * TILES + i : c * TILES + i + 1]
+                sums = res_tiles[c][:, i, :]
+                if s == 0:
+                    nc.vector.tensor_scalar(
+                        out=sums, in0=f_ps_tiles[k][:, i, :], scalar1=weight, scalar2=None, op0=ALU.mult
+                    )
+                else:
+                    nc.vector.scalar_tensor_tensor(
+                        out=sums,
+                        in0=f_ps_tiles[k][:, i, :],
+                        scalar=weight,
+                        in1=sums,
+                        op0=ALU.mult,
+                        op1=ALU.add,
+                    )
 
         def chunk_due(k, lead):
             c, s = divmod(k + lead, S)
@@ -265,12 +262,13 @@ def tile_moe_pb_e_kernel(
                 quantise_h1(k - QUANTISE_LAG)
             if 0 <= k - REGROUP_LAG < STEPS:
                 regroup_h1(k - REGROUP_LAG)
-            if 0 <= k - TRANSPOSE_LAG < N_TILES:
+            if 0 <= k - TRANSPOSE_LAG < STEPS:
                 transpose_probs(k - TRANSPOSE_LAG)
-            if 0 <= k - WEIGH_LAG < N_TILES:
+            if 0 <= k - WEIGH_LAG < STEPS:
                 weigh(k - WEIGH_LAG)
-            if 0 <= k - STORE_LAG < N_TILES:
-                nc.sync.dma_start(out=out_tiles[k - STORE_LAG], in_=res_tiles[k - STORE_LAG][:])
+            if 0 <= k - STORE_LAG < STEPS and (k - STORE_LAG) % S == S - 1:
+                c = (k - STORE_LAG) // S
+                nc.sync.dma_start(out=out_chunks[c], in_=res_tiles[c][:])
             c = chunk_due(k, H0_RELU_LEAD)
             if c is not None:
                 relu_h0(c)

@@ -35,6 +35,7 @@ H0_COPY_LEAD = (4, 2)
 H0_TRANSPOSE_LEAD = (5, 3)
 H0_RELU_LEAD = 6
 LOAD_LEAD = 12
+HEAD_STEPS = 2
 
 FLOPS = 2 * S * N_TOKENS * H * (H + T)
 
@@ -68,6 +69,7 @@ def tile_moe_pb_e_kernel(
 
         rows = const.tile([P, H + T], BF16, name="rows")
         nc.vector.memset(rows[:], 0.0)
+        alpha_rows = const.tile([P, P], BF16, name="alpha_rows")
         w1_planes_in = const.tile([P, H], U8, name="w1_planes_in", align_bytes=64)
         w2_planes = const.tile([P, T], U8, name="w2_planes", align_bytes=64)
         nc.vector.memset(w1_planes_in[:].bitcast(I32), 0)
@@ -75,49 +77,79 @@ def tile_moe_pb_e_kernel(
         identity = const.tile([P, P], F32, name="identity")
         make_identity(nc, identity[:])
 
+        def load_planes(planes, scales):
+            for quadrant in range(4):
+                nc.sync.dma_start(
+                    out=planes[32 * quadrant : 32 * quadrant + 16, :].bitcast(I32),
+                    in_=scales[:, 4 * quadrant : 4 * quadrant + 4, :].bitcast(I32),
+                )
+
+        w1_in = const.tile([P, S, H], I32, name="w1_in", align_bytes=64)
+
+        def load_w1(s):
+            nc.sync.dma_start(
+                out=w1_in[:, s, :], in_=W1_words[s].rearrange("p n t -> p (n t)").bitcast(I32)
+            )
+
         enc_tiles = {0: load_chunk(0)}
         nc.sync.dma_start(out=rows[0:S, 0:H], in_=b1)
         nc.sync.dma_start(out=rows[0:S, H : H + T], in_=b2)
-        for quadrant in range(4):
-            nc.sync.dma_start(
-                out=w1_planes_in[32 * quadrant : 32 * quadrant + 16, :].bitcast(I32),
-                in_=W1_scales[:, 4 * quadrant : 4 * quadrant + 4, :].bitcast(I32),
-            )
-        w1_in = const.tile([P, S, H], I32, name="w1_in", align_bytes=64)
-        for s in range(S):
-            nc.sync.dma_start(
-                out=w1_in[:, s, :],
-                in_=W1_words[s].rearrange("p n t -> p (n t)").bitcast(I32),
-            )
-        alpha_rows = const.tile([P, P], BF16, name="alpha_rows")
         nc.sync.dma_start(out=alpha_rows[:], in_=alphas.rearrange("s (j p) -> (s j) p", p=P))
-        for quadrant in range(4):
-            nc.sync.dma_start(
-                out=w2_planes[32 * quadrant : 32 * quadrant + 16, :].bitcast(I32),
-                in_=W2_scales[:, 4 * quadrant : 4 * quadrant + 4, :].bitcast(I32),
-            )
+        load_planes(w1_planes_in, W1_scales)
+        load_w1(0)
+        enc_tiles[1] = load_chunk(1)
+        for s in range(1, S):
+            load_w1(s)
+        load_planes(w2_planes, W2_scales)
         w2_words = const.tile([P, S, T], I32, name="w2_words", align_bytes=64)
         nc.sync.dma_start(
             out=w2_words[:], in_=W2_words.rearrange("g p n t -> p g (n t)").bitcast(I32)
         )
-        enc_tiles[1] = load_chunk(1)
         enc_tiles[2] = load_chunk(2)
 
-        rows_f32 = const.tile([P, H_TILES + 1, P], F32, name="rows_f32")
-        nc.vector.tensor_copy(
-            out=rows_f32[:, 0:H_TILES, :].rearrange("p tau (a i) -> p tau a i", i=PACK),
-            in_=rows[:, 0:H].rearrange("p (a tau i) -> p tau a i", tau=H_TILES, i=PACK),
-        )
-        nc.vector.tensor_copy(out=rows_f32[:, H_TILES, :], in_=rows[:, H : H + T])
-        b1_ps = psum_f.tile([P, H_TILES, P], F32, name="f_ps")
-        for tau in range(H_TILES):
-            nc.tensor.transpose(b1_ps[:, tau, :], rows_f32[:, tau, :], identity[:])
-        b2_ps = psum_f.tile([P, H_TILES, P], F32, name="f_ps")
-        nc.tensor.transpose(b2_ps[:, 0, :], rows_f32[:, H_TILES, :], identity[:])
+        w1_planes = const.tile([P, H_TILES, P], U8, name="w1_planes", align_bytes=64)
+        w1_tiles = const.tile([P, S, H_TILES, P], I32, name="w1_tiles", align_bytes=64)
+
+        def sort_w1_planes():
+            nc.vector.tensor_copy(
+                out=w1_planes[:].bitcast(I32),
+                in_=w1_planes_in[:].bitcast(I32).rearrange("p (a tau) -> p tau a", tau=H_TILES),
+            )
+
+        def sort_w1(s):
+            nc.vector.tensor_copy(
+                out=w1_tiles[:, s, :, :].rearrange("p tau (a i) -> p tau a i", i=PACK),
+                in_=w1_in[:, s, :].rearrange("p (a tau i) -> p tau a i", tau=H_TILES, i=PACK),
+            )
+
+        SMALL_BLOCKS = H_TILES + 2
+        small_rows = const.tile([P, SMALL_BLOCKS, P], F32, name="small_rows")
         b1_cols = const.tile([P, H_TILES, S], F32, name="b1_cols")
-        nc.vector.tensor_copy(out=b1_cols[:], in_=b1_ps[:, :, 0:S])
         b2_cols = const.tile([P, S], F32, name="b2_cols")
-        nc.vector.tensor_copy(out=b2_cols[:], in_=b2_ps[:, 0, 0:S])
+        alpha_cols = const.tile([P, S, N_TILES], F32, name="alpha_cols")
+        small_ps = {}
+
+        def widen_small_rows():
+            nc.vector.tensor_copy(
+                out=small_rows[:, 0:H_TILES, :].rearrange("p tau (a i) -> p tau a i", i=PACK),
+                in_=rows[:, 0:H].rearrange("p (a tau i) -> p tau a i", tau=H_TILES, i=PACK),
+            )
+            nc.vector.tensor_copy(out=small_rows[:, H_TILES, :], in_=rows[:, H : H + T])
+            nc.vector.tensor_copy(out=small_rows[:, H_TILES + 1, :], in_=alpha_rows[:])
+
+        def transpose_small_rows():
+            for bank in range(2):
+                small_ps[bank] = psum_f.tile([P, H_TILES, P], F32, name="f_ps")
+            for block in range(SMALL_BLOCKS):
+                bank, place = divmod(block, H_TILES)
+                nc.tensor.transpose(small_ps[bank][:, place, :], small_rows[:, block, :], identity[:])
+
+        def keep_small_columns():
+            nc.vector.tensor_copy(out=b1_cols[:], in_=small_ps[0][:, :, 0:S])
+            nc.vector.tensor_copy(out=b2_cols[:], in_=small_ps[1][:, 0, 0:S])
+            nc.vector.tensor_copy(
+                out=alpha_cols[:].rearrange("p s j -> p (s j)"), in_=small_ps[1][:, 1, :]
+            )
 
         h0_tiles = {}
         h0_grouped_tiles = {}
@@ -178,9 +210,13 @@ def tile_moe_pb_e_kernel(
                     stop=True,
                 )
                 y = y_pool.tile([P, CHUNK], BF16, name="y")
-                nc.scalar.activation(
-                    out=y[:], in_=x_ps[:], func=ACT.Relu, bias=b1_cols[:, tau, s : s + 1], scale=1.0
-                )
+                bias = b1_cols[:, tau, s : s + 1]
+                if k < HEAD_STEPS and tau % 2 == 1:
+                    nc.vector.tensor_scalar(
+                        out=y[:], in0=x_ps[:], scalar1=bias, scalar2=0.0, op0=ALU.add, op1=ALU.max
+                    )
+                else:
+                    nc.scalar.activation(out=y[:], in_=x_ps[:], func=ACT.Relu, bias=bias, scale=1.0)
                 nc.sync.dma_start(out=planes[tau:P:H_TILES, :, :], in_=y[:])
             planes_tiles[k] = planes
 
@@ -256,6 +292,8 @@ def tile_moe_pb_e_kernel(
                 enc_tiles[c] = load_chunk(c)
             if 0 <= k < STEPS:
                 layer1(k)
+            if k + 2 < S:
+                sort_w1(k + 2)
             if 0 <= k - LAYER2_LAG < STEPS:
                 layer2(k - LAYER2_LAG)
             if 0 <= k - QUANTISE_LAG < STEPS:
@@ -283,29 +321,20 @@ def tile_moe_pb_e_kernel(
             if c is not None:
                 quantise_h0(c)
 
-        for k in range(-H0_RELU_LEAD, 0):
-            step(k)
-
-        w1_planes = const.tile([P, H_TILES, P], U8, name="w1_planes", align_bytes=64)
-        nc.vector.tensor_copy(
-            out=w1_planes[:].bitcast(I32),
-            in_=w1_planes_in[:].bitcast(I32).rearrange("p (a tau) -> p tau a", tau=H_TILES),
-        )
-        w1_tiles = const.tile([P, S, H_TILES, P], I32, name="w1_tiles", align_bytes=64)
-        for s in range(S):
-            nc.vector.tensor_copy(
-                out=w1_tiles[:, s, :, :].rearrange("p tau (a i) -> p tau a i", i=PACK),
-                in_=w1_in[:, s, :].rearrange("p (a tau i) -> p tau a i", tau=H_TILES, i=PACK),
-            )
-
-        alpha_f32 = const.tile([P, P], F32, name="alpha_f32")
-        nc.vector.tensor_copy(out=alpha_f32[:], in_=alpha_rows[:])
-        alpha_ps = psum_f.tile([P, H_TILES, P], F32, name="f_ps")
-        nc.tensor.transpose(alpha_ps[:, 0, :], alpha_f32[:], identity[:])
-        alpha_cols = const.tile([P, S, N_TILES], F32, name="alpha_cols")
-        nc.vector.tensor_copy(
-            out=alpha_cols[:].rearrange("p s j -> p (s j)"), in_=alpha_ps[:, 0, :]
-        )
+        relu_h0(0)
+        transpose_h0(0, 0)
+        widen_small_rows()
+        sort_w1_planes()
+        transpose_small_rows()
+        copy_h0(0, 0)
+        transpose_h0(0, 1)
+        sort_w1(0)
+        keep_small_columns()
+        relu_h0(1)
+        copy_h0(0, 1)
+        transpose_h0(1, 0)
+        quantise_h0(0)
+        sort_w1(1)
 
         for k in range(STEPS + STORE_LAG):
             step(k)

@@ -181,7 +181,8 @@ def tile_moe_pb_e_kernel(
             grouped_words = h0_grouped_tiles[c][:].bitcast(F32).rearrange(
                 "p (i n u) -> p i n u", i=TILES, u=2
             )
-            nc.vector.tensor_copy(
+            copy = nc.vector.tensor_copy if half == 0 else nc.scalar.copy
+            copy(
                 out=grouped_words[:, 2 * half : 2 * half + 2, :, :],
                 in_=e_ps_tiles[c, half][:].rearrange("p i u n -> p i n u"),
             )

@@ -19,10 +19,13 @@ S = 4
 T = 128
 CHUNK = 512
 TILES = CHUNK // P
+HALF = TILES // 2
 N_CHUNKS = N_TOKENS // CHUNK
 N_TILES = N_TOKENS // P
 H_TILES = H // P
 STEPS = N_CHUNKS * S
+QUADRANTS = 4
+RUN = 4
 
 REGROUP_LAG = 3
 QUANTISE_LAG = REGROUP_LAG + 1
@@ -33,8 +36,7 @@ STORE_LAG = WEIGH_LAG + 1
 H0_QUANTISE_LEAD = 1
 H0_COPY_LEAD = (4, 2)
 H0_TRANSPOSE_LEAD = (5, 3)
-H0_RELU_LEAD = 6
-LOAD_LEAD = 12
+LOAD_LEAD = 3 * S
 HEAD_STEPS = 2
 
 FLOPS = 2 * S * N_TOKENS * H * (H + T)
@@ -44,8 +46,8 @@ def tile_moe_pb_e_kernel(
     tc, encodings, alphas, W1_words, W1_scales, b1, W2_words, W2_scales, b2, out
 ):
     nc = tc.nc
-    enc_chunks = encodings.rearrange("(c i p) h -> c p i h", i=TILES, p=P)
-    out_chunks = out.rearrange("(c i p) t -> c p i t", i=TILES, p=P)
+    enc_chunks = encodings.rearrange("(c m p) h -> c p m h", m=TILES, p=P)
+    out_chunks = out.rearrange("(c m p) o -> c p m o", m=TILES, p=P)
 
     with ExitStack() as ctx:
         ctx.enter_context(tc.manual_schedule())
@@ -53,10 +55,10 @@ def tile_moe_pb_e_kernel(
         enc_pool = ctx.enter_context(tc.tile_pool(name="enc", bufs=4))
         h0_pool = ctx.enter_context(tc.tile_pool(name="h0", bufs=2))
         y_pool = ctx.enter_context(tc.tile_pool(name="y", bufs=2 * H_TILES))
-        planes_pool = ctx.enter_context(tc.tile_pool(name="planes", bufs=REGROUP_LAG + 2))
+        sheets_pool = ctx.enter_context(tc.tile_pool(name="sheets", bufs=REGROUP_LAG + 2))
         h1_pool = ctx.enter_context(tc.tile_pool(name="h1", bufs=3))
         prob_pool = ctx.enter_context(tc.tile_pool(name="prob", bufs=3))
-        res_pool = ctx.enter_context(tc.tile_pool(name="res", bufs=2))
+        sums_pool = ctx.enter_context(tc.tile_pool(name="sums", bufs=2))
         psum_x = ctx.enter_context(tc.psum_pool(name="psum_x", bufs=4))
         psum_e = ctx.enter_context(tc.psum_pool(name="psum_e", bufs=1))
         psum_z = ctx.enter_context(tc.psum_pool(name="psum_z", bufs=1))
@@ -67,8 +69,8 @@ def tile_moe_pb_e_kernel(
             nc.sync.dma_start(out=enc_sb[:], in_=enc_chunks[c])
             return enc_sb
 
-        rows = const.tile([P, H + T], BF16, name="rows")
-        nc.vector.memset(rows[:], 0.0)
+        bias_rows = const.tile([P, H + T], BF16, name="bias_rows")
+        nc.vector.memset(bias_rows[:], 0.0)
         alpha_rows = const.tile([P, P], BF16, name="alpha_rows")
         w1_planes_in = const.tile([P, H], U8, name="w1_planes_in", align_bytes=64)
         w2_planes = const.tile([P, T], U8, name="w2_planes", align_bytes=64)
@@ -78,9 +80,9 @@ def tile_moe_pb_e_kernel(
         make_identity(nc, identity[:])
 
         def load_planes(planes, scales):
-            for quadrant in range(4):
+            for quadrant in range(QUADRANTS):
                 nc.sync.dma_start(
-                    out=planes[32 * quadrant : 32 * quadrant + 16, :].bitcast(I32),
+                    out=planes[32 * quadrant : 32 * quadrant + 4 * S, :].bitcast(I32),
                     in_=scales[:, 4 * quadrant : 4 * quadrant + 4, :].bitcast(I32),
                 )
 
@@ -88,12 +90,12 @@ def tile_moe_pb_e_kernel(
 
         def load_w1(s):
             nc.sync.dma_start(
-                out=w1_in[:, s, :], in_=W1_words[s].rearrange("p n t -> p (n t)").bitcast(I32)
+                out=w1_in[:, s, :], in_=W1_words[s].rearrange("p col t -> p (col t)").bitcast(I32)
             )
 
         enc_tiles = {0: load_chunk(0)}
-        nc.sync.dma_start(out=rows[0:S, 0:H], in_=b1)
-        nc.sync.dma_start(out=rows[0:S, H : H + T], in_=b2)
+        nc.sync.dma_start(out=bias_rows[0:S, 0:H], in_=b1)
+        nc.sync.dma_start(out=bias_rows[0:S, H : H + T], in_=b2)
         nc.sync.dma_start(out=alpha_rows[:], in_=alphas.rearrange("s (j p) -> (s j) p", p=P))
         load_planes(w1_planes_in, W1_scales)
         load_w1(0)
@@ -103,7 +105,7 @@ def tile_moe_pb_e_kernel(
         load_planes(w2_planes, W2_scales)
         w2_words = const.tile([P, S, T], I32, name="w2_words", align_bytes=64)
         nc.sync.dma_start(
-            out=w2_words[:], in_=W2_words.rearrange("g p n t -> p g (n t)").bitcast(I32)
+            out=w2_words[:], in_=W2_words.rearrange("s p col t -> p s (col t)").bitcast(I32)
         )
         enc_tiles[2] = load_chunk(2)
 
@@ -122,8 +124,8 @@ def tile_moe_pb_e_kernel(
                 in_=w1_in[:, s, :].rearrange("p (a tau i) -> p tau a i", tau=H_TILES, i=PACK),
             )
 
-        SMALL_BLOCKS = H_TILES + 2
-        small_rows = const.tile([P, SMALL_BLOCKS, P], F32, name="small_rows")
+        strips = H_TILES + 2
+        small_rows = const.tile([P, strips, P], F32, name="small_rows")
         b1_cols = const.tile([P, H_TILES, S], F32, name="b1_cols")
         b2_cols = const.tile([P, S], F32, name="b2_cols")
         alpha_cols = const.tile([P, S, N_TILES], F32, name="alpha_cols")
@@ -132,17 +134,17 @@ def tile_moe_pb_e_kernel(
         def widen_small_rows():
             nc.vector.tensor_copy(
                 out=small_rows[:, 0:H_TILES, :].rearrange("p tau (a i) -> p tau a i", i=PACK),
-                in_=rows[:, 0:H].rearrange("p (a tau i) -> p tau a i", tau=H_TILES, i=PACK),
+                in_=bias_rows[:, 0:H].rearrange("p (a tau i) -> p tau a i", tau=H_TILES, i=PACK),
             )
-            nc.vector.tensor_copy(out=small_rows[:, H_TILES, :], in_=rows[:, H : H + T])
+            nc.vector.tensor_copy(out=small_rows[:, H_TILES, :], in_=bias_rows[:, H : H + T])
             nc.vector.tensor_copy(out=small_rows[:, H_TILES + 1, :], in_=alpha_rows[:])
 
         def transpose_small_rows():
             for bank in range(2):
                 small_ps[bank] = psum_f.tile([P, H_TILES, P], F32, name="f_ps")
-            for block in range(SMALL_BLOCKS):
-                bank, place = divmod(block, H_TILES)
-                nc.tensor.transpose(small_ps[bank][:, place, :], small_rows[:, block, :], identity[:])
+            for strip in range(strips):
+                bank, place = divmod(strip, H_TILES)
+                nc.tensor.transpose(small_ps[bank][:, place, :], small_rows[:, strip, :], identity[:])
 
         def keep_small_columns():
             nc.vector.tensor_copy(out=b1_cols[:], in_=small_ps[0][:, :, 0:S])
@@ -151,41 +153,38 @@ def tile_moe_pb_e_kernel(
                 out=alpha_cols[:].rearrange("p s j -> p (s j)"), in_=small_ps[1][:, 1, :]
             )
 
-        h0_tiles = {}
         h0_grouped_tiles = {}
         e_ps_tiles = {}
         h0_operands = {}
-        planes_tiles = {}
+        sheets_tiles = {}
         h1_grouped_tiles = {}
         h1_operands = {}
         prob_tiles = {}
         f_ps_tiles = {}
-        res_tiles = {}
-
-        def relu_h0(c):
-            h0_tiles[c] = h0_pool.tile([P, TILES, H], BF16, name="h0")
-            nc.vector.tensor_scalar_max(out=h0_tiles[c][:], in0=enc_tiles[c][:], scalar1=0.0)
-            h0_grouped_tiles[c] = h0_pool.tile(
-                [P, CHUNK * PACK], BF16, name="h0_grouped", align_bytes=64
-            )
+        sums_tiles = {}
 
         def transpose_h0(c, half):
-            e_ps = psum_e.tile([P, 2, 2, P], F32, name="e_ps")
-            for i in range(2):
-                words = h0_tiles[c][:, 2 * half + i, :].bitcast(F32)
+            e_ps = psum_e.tile([P, HALF, 2, P], F32, name="e_ps")
+            for m in range(HALF):
+                pairs = enc_tiles[c][:, HALF * half + m, :].bitcast(F32)
                 for u in range(2):
-                    nc.tensor.transpose(e_ps[:, i, u, :], words[:, u : H // 2 : 2], identity[:])
+                    nc.tensor.transpose(e_ps[:, m, u, :], pairs[:, u : H // 2 : 2], identity[:])
             e_ps_tiles[c, half] = e_ps
 
-        def copy_h0(c, half):
-            grouped_words = h0_grouped_tiles[c][:].bitcast(F32).rearrange(
-                "p (i n u) -> p i n u", i=TILES, u=2
-            )
-            copy = nc.vector.tensor_copy if half == 0 else nc.scalar.copy
-            copy(
-                out=grouped_words[:, 2 * half : 2 * half + 2, :, :],
-                in_=e_ps_tiles[c, half][:].rearrange("p i u n -> p i n u"),
-            )
+        def relu_h0(c, half):
+            if half == 0:
+                h0_grouped_tiles[c] = h0_pool.tile(
+                    [P, CHUNK * PACK], BF16, name="h0_grouped", align_bytes=64
+                )
+            grouped = h0_grouped_tiles[c][:].rearrange("p (m n u e) -> p m n u e", m=TILES, u=2, e=2)
+            for m in range(HALF):
+                nc.vector.tensor_scalar_max(
+                    out=grouped[:, HALF * half + m, :, :, :],
+                    in0=e_ps_tiles[c, half][:, m, :, :]
+                    .bitcast(BF16)
+                    .rearrange("p u (n e) -> p n u e", e=2),
+                    scalar1=0.0,
+                )
 
         def quantise_h0(c):
             h0_codes = h0_pool.tile([P, CHUNK], I32, name="h0_codes", align_bytes=64)
@@ -195,10 +194,10 @@ def tile_moe_pb_e_kernel(
             )
             h0_operands[c] = (h0_codes, h0_plane)
 
-        def layer1(k):
-            c, s = divmod(k, S)
+        def layer1(step):
+            c, s = divmod(step, S)
             h0_codes, h0_plane = h0_operands[c]
-            planes = planes_pool.tile([P, PACK, CHUNK], BF16, name="planes")
+            sheets = sheets_pool.tile([P, PACK, CHUNK], BF16, name="sheets")
             for tau in range(H_TILES):
                 x_ps = psum_x.tile([P, CHUNK], F32, name="x_ps")
                 nc.tensor.matmul_mx(
@@ -212,34 +211,34 @@ def tile_moe_pb_e_kernel(
                 )
                 y = y_pool.tile([P, CHUNK], BF16, name="y")
                 bias = b1_cols[:, tau, s : s + 1]
-                if k < HEAD_STEPS and tau % 2 == 1:
+                if step < HEAD_STEPS and tau % 2 == 1:
                     nc.vector.tensor_scalar(
                         out=y[:], in0=x_ps[:], scalar1=bias, scalar2=0.0, op0=ALU.add, op1=ALU.max
                     )
                 else:
                     nc.scalar.activation(out=y[:], in_=x_ps[:], func=ACT.Relu, bias=bias, scale=1.0)
-                nc.sync.dma_start(out=planes[tau:P:H_TILES, :, :], in_=y[:])
-            planes_tiles[k] = planes
+                nc.sync.dma_start(out=sheets[tau:P:H_TILES, :, :], in_=y[:])
+            sheets_tiles[step] = sheets
 
-        def regroup_h1(k):
+        def regroup_h1(step):
             h1_grouped = h1_pool.tile([P, CHUNK * PACK], BF16, name="h1_grouped", align_bytes=64)
             nc.vector.tensor_copy(
-                out=h1_grouped[:].rearrange("p (c i t) -> p c t i", i=4, t=PACK),
-                in_=planes_tiles[k][:].rearrange("p t (c i) -> p c t i", i=4),
+                out=h1_grouped[:].rearrange("p (run r t) -> p run t r", r=RUN, t=PACK),
+                in_=sheets_tiles[step][:].rearrange("p t (run r) -> p run t r", r=RUN),
             )
-            h1_grouped_tiles[k] = h1_grouped
+            h1_grouped_tiles[step] = h1_grouped
 
-        def quantise_h1(k):
+        def quantise_h1(step):
             h1_codes = h1_pool.tile([P, CHUNK], I32, name="h1_codes", align_bytes=64)
             h1_plane = h1_pool.tile([P, CHUNK], U8, name="h1_plane", align_bytes=64)
             nc.vector.quantize_mx(
-                out=h1_codes[:].bitcast(FP8X4), scales=h1_plane[:], in_=h1_grouped_tiles[k][:]
+                out=h1_codes[:].bitcast(FP8X4), scales=h1_plane[:], in_=h1_grouped_tiles[step][:]
             )
-            h1_operands[k] = (h1_codes, h1_plane)
+            h1_operands[step] = (h1_codes, h1_plane)
 
-        def layer2(k):
-            s = k % S
-            h1_codes, h1_plane = h1_operands[k]
+        def layer2(step):
+            s = step % S
+            h1_codes, h1_plane = h1_operands[step]
             z_ps = psum_z.tile([P, CHUNK], F32, name="z_ps")
             nc.tensor.matmul_mx(
                 out=z_ps[:],
@@ -254,88 +253,83 @@ def tile_moe_pb_e_kernel(
             nc.scalar.activation(
                 out=prob[:], in_=z_ps[:], func=ACT.Sigmoid, bias=b2_cols[:, s : s + 1], scale=1.0
             )
-            prob_tiles[k] = prob
+            prob_tiles[step] = prob
 
-        def transpose_probs(k):
+        def transpose_probs(step):
             f_ps = psum_f.tile([P, TILES, T], F32, name="f_ps")
-            for i in range(TILES):
-                nc.tensor.transpose(f_ps[:, i, :], prob_tiles[k][:, i * P : (i + 1) * P], identity[:])
-            f_ps_tiles[k] = f_ps
+            for m in range(TILES):
+                nc.tensor.transpose(f_ps[:, m, :], prob_tiles[step][:, m * P : (m + 1) * P], identity[:])
+            f_ps_tiles[step] = f_ps
 
-        def weigh(k):
-            c, s = divmod(k, S)
+        def weigh(step):
+            c, s = divmod(step, S)
             if s == 0:
-                res_tiles[c] = res_pool.tile([P, TILES, T], F32, name="res")
-            for i in range(TILES):
-                weight = alpha_cols[:, s, c * TILES + i : c * TILES + i + 1]
-                sums = res_tiles[c][:, i, :]
+                sums_tiles[c] = sums_pool.tile([P, TILES, T], F32, name="sums")
+            for m in range(TILES):
+                weight = alpha_cols[:, s, c * TILES + m : c * TILES + m + 1]
+                sums = sums_tiles[c][:, m, :]
                 if s == 0:
                     nc.vector.tensor_scalar(
-                        out=sums, in0=f_ps_tiles[k][:, i, :], scalar1=weight, scalar2=None, op0=ALU.mult
+                        out=sums, in0=f_ps_tiles[step][:, m, :], scalar1=weight, scalar2=None, op0=ALU.mult
                     )
                 else:
                     nc.vector.scalar_tensor_tensor(
                         out=sums,
-                        in0=f_ps_tiles[k][:, i, :],
+                        in0=f_ps_tiles[step][:, m, :],
                         scalar=weight,
                         in1=sums,
                         op0=ALU.mult,
                         op1=ALU.add,
                     )
 
-        def chunk_due(k, lead):
-            c, s = divmod(k + lead, S)
+        def chunk_due(step, lead):
+            c, s = divmod(step + lead, S)
             return c if s == 0 and 0 <= c < N_CHUNKS else None
 
-        def step(k):
-            c = chunk_due(k, LOAD_LEAD)
-            if c is not None and c not in enc_tiles:
-                enc_tiles[c] = load_chunk(c)
-            if 0 <= k < STEPS:
-                layer1(k)
-            if k + 2 < S:
-                sort_w1(k + 2)
-            if 0 <= k - LAYER2_LAG < STEPS:
-                layer2(k - LAYER2_LAG)
-            if 0 <= k - QUANTISE_LAG < STEPS:
-                quantise_h1(k - QUANTISE_LAG)
-            if 0 <= k - REGROUP_LAG < STEPS:
-                regroup_h1(k - REGROUP_LAG)
-            if 0 <= k - TRANSPOSE_LAG < STEPS:
-                transpose_probs(k - TRANSPOSE_LAG)
-            if 0 <= k - WEIGH_LAG < STEPS:
-                weigh(k - WEIGH_LAG)
-            if 0 <= k - STORE_LAG < STEPS and (k - STORE_LAG) % S == S - 1:
-                c = (k - STORE_LAG) // S
-                nc.sync.dma_start(out=out_chunks[c], in_=res_tiles[c][:])
-            c = chunk_due(k, H0_RELU_LEAD)
+        def write_step(step):
+            c = chunk_due(step, LOAD_LEAD)
             if c is not None:
-                relu_h0(c)
+                enc_tiles[c] = load_chunk(c)
+            if step < STEPS:
+                layer1(step)
+            if step + 2 < S:
+                sort_w1(step + 2)
+            if 0 <= step - LAYER2_LAG < STEPS:
+                layer2(step - LAYER2_LAG)
+            if 0 <= step - QUANTISE_LAG < STEPS:
+                quantise_h1(step - QUANTISE_LAG)
+            if 0 <= step - REGROUP_LAG < STEPS:
+                regroup_h1(step - REGROUP_LAG)
+            if 0 <= step - TRANSPOSE_LAG < STEPS:
+                transpose_probs(step - TRANSPOSE_LAG)
+            if 0 <= step - WEIGH_LAG < STEPS:
+                weigh(step - WEIGH_LAG)
+            if 0 <= step - STORE_LAG < STEPS and (step - STORE_LAG) % S == S - 1:
+                c = (step - STORE_LAG) // S
+                nc.sync.dma_start(out=out_chunks[c], in_=sums_tiles[c][:])
             for half in range(2):
-                c = chunk_due(k, H0_TRANSPOSE_LEAD[half])
+                c = chunk_due(step, H0_TRANSPOSE_LEAD[half])
                 if c is not None:
                     transpose_h0(c, half)
-                c = chunk_due(k, H0_COPY_LEAD[half])
+                c = chunk_due(step, H0_COPY_LEAD[half])
                 if c is not None:
-                    copy_h0(c, half)
-            c = chunk_due(k, H0_QUANTISE_LEAD)
+                    relu_h0(c, half)
+            c = chunk_due(step, H0_QUANTISE_LEAD)
             if c is not None:
                 quantise_h0(c)
 
-        relu_h0(0)
         transpose_h0(0, 0)
         widen_small_rows()
         sort_w1_planes()
         transpose_small_rows()
-        copy_h0(0, 0)
+        relu_h0(0, 0)
         transpose_h0(0, 1)
         sort_w1(0)
         keep_small_columns()
-        relu_h0(1)
-        copy_h0(0, 1)
+        relu_h0(0, 1)
         transpose_h0(1, 0)
         quantise_h0(0)
         sort_w1(1)
 
-        for k in range(STEPS + STORE_LAG):
-            step(k)
+        for step in range(STEPS + STORE_LAG):
+            write_step(step)

@@ -78,6 +78,9 @@ def tile_moe_pb_e_kernel(
         nc.vector.memset(w2_planes[:].bitcast(I32), 0)
         identity = const.tile([P, P], F32, name="identity")
         make_identity(nc, identity[:])
+        warm = const.tile([P, 2], F32, name="warm")
+        nc.gpsimd.memset(warm[:, 0:1], 0.0)
+        nc.scalar.activation(out=warm[:, 1:2], in_=warm[:, 0:1], func=ACT.Sigmoid)
 
         def load_planes(planes, scales):
             for quadrant in range(QUADRANTS):

@@ -27,7 +27,7 @@ STEPS = N_CHUNKS * S
 QUADRANTS = 4
 RUN = 4
 
-REGROUP_LAG = 3
+REGROUP_LAG = 2
 QUANTISE_LAG = REGROUP_LAG + 1
 LAYER2_LAG = QUANTISE_LAG + 1
 TRANSPOSE_LAG = LAYER2_LAG + 1
@@ -66,7 +66,11 @@ def tile_moe_pb_e_kernel(
 
         def load_chunk(c):
             enc_sb = enc_pool.tile([P, TILES, H], BF16, name="enc_sb")
-            nc.sync.dma_start(out=enc_sb[:], in_=enc_chunks[c])
+            if c == 0:
+                for m in range(TILES):
+                    nc.sync.dma_start(out=enc_sb[:, m, :], in_=enc_chunks[c][:, m, :])
+            else:
+                nc.sync.dma_start(out=enc_sb[:], in_=enc_chunks[c])
             return enc_sb
 
         bias_rows = const.tile([P, H + T], BF16, name="bias_rows")
@@ -102,8 +106,9 @@ def tile_moe_pb_e_kernel(
         nc.sync.dma_start(out=alpha_rows[:], in_=alphas.rearrange("s (j p) -> (s j) p", p=P))
         load_planes(w1_planes_in, W1_scales)
         load_w1(0)
+        load_w1(1)
         enc_tiles[1] = load_chunk(1)
-        for s in range(1, S):
+        for s in range(2, S):
             load_w1(s)
         load_planes(w2_planes, W2_scales)
         w2_words = const.tile([P, S, T], I32, name="w2_words", align_bytes=64)
@@ -135,12 +140,12 @@ def tile_moe_pb_e_kernel(
         small_ps = {}
 
         def widen_small_rows():
-            nc.vector.tensor_copy(
+            nc.scalar.copy(
                 out=small_rows[:, 0:H_TILES, :].rearrange("p tau (a i) -> p tau a i", i=PACK),
                 in_=bias_rows[:, 0:H].rearrange("p (a tau i) -> p tau a i", tau=H_TILES, i=PACK),
             )
-            nc.vector.tensor_copy(out=small_rows[:, H_TILES, :], in_=bias_rows[:, H : H + T])
-            nc.vector.tensor_copy(out=small_rows[:, H_TILES + 1, :], in_=alpha_rows[:])
+            nc.scalar.copy(out=small_rows[:, H_TILES, :], in_=bias_rows[:, H : H + T])
+            nc.scalar.copy(out=small_rows[:, H_TILES + 1, :], in_=alpha_rows[:])
 
         def transpose_small_rows():
             for bank in range(2):
@@ -150,11 +155,9 @@ def tile_moe_pb_e_kernel(
                 nc.tensor.transpose(small_ps[bank][:, place, :], small_rows[:, strip, :], identity[:])
 
         def keep_small_columns():
-            nc.vector.tensor_copy(out=b1_cols[:], in_=small_ps[0][:, :, 0:S])
-            nc.vector.tensor_copy(out=b2_cols[:], in_=small_ps[1][:, 0, 0:S])
-            nc.vector.tensor_copy(
-                out=alpha_cols[:].rearrange("p s j -> p (s j)"), in_=small_ps[1][:, 1, :]
-            )
+            nc.scalar.copy(out=b1_cols[:], in_=small_ps[0][:, :, 0:S])
+            nc.scalar.copy(out=b2_cols[:], in_=small_ps[1][:, 0, 0:S])
+            nc.scalar.copy(out=alpha_cols[:].rearrange("p s j -> p (s j)"), in_=small_ps[1][:, 1, :])
 
         h0_grouped_tiles = {}
         e_ps_tiles = {}
@@ -167,7 +170,12 @@ def tile_moe_pb_e_kernel(
         sums_tiles = {}
 
         def transpose_h0(c, half):
-            e_ps = psum_e.tile([P, HALF, 2, P], F32, name="e_ps")
+            if c == 0 and half == 1:
+                x_ps = psum_x.tile([P, CHUNK], F32, name="x_ps")
+                e_ps = x_ps[:].rearrange("p (m u n) -> p m u n", m=HALF, u=2)
+            else:
+                e_tile = psum_e.tile([P, HALF, 2, P], F32, name="e_ps")
+                e_ps = e_tile[:]
             for m in range(HALF):
                 pairs = enc_tiles[c][:, HALF * half + m, :].bitcast(F32)
                 for u in range(2):
@@ -253,16 +261,27 @@ def tile_moe_pb_e_kernel(
                 stop=True,
             )
             prob = prob_pool.tile([P, CHUNK], F32, name="prob")
-            nc.scalar.activation(
-                out=prob[:], in_=z_ps[:], func=ACT.Sigmoid, bias=b2_cols[:, s : s + 1], scale=1.0
-            )
+            pieces = TILES if step == STEPS - 1 else 1
+            width = CHUNK // pieces
+            for i in range(pieces):
+                cols = slice(i * width, (i + 1) * width)
+                nc.scalar.activation(
+                    out=prob[:, cols], in_=z_ps[:, cols], func=ACT.Sigmoid, bias=b2_cols[:, s : s + 1], scale=1.0
+                )
             prob_tiles[step] = prob
 
         def transpose_probs(step):
-            f_ps = psum_f.tile([P, TILES, T], F32, name="f_ps")
+            if step == STEPS - 1:
+                views = []
+                for m in range(TILES):
+                    x_ps = psum_x.tile([P, CHUNK], F32, name="x_ps")
+                    views.append(x_ps[:, 0:T])
+            else:
+                f_ps = psum_f.tile([P, TILES, T], F32, name="f_ps")
+                views = [f_ps[:, m, :] for m in range(TILES)]
             for m in range(TILES):
-                nc.tensor.transpose(f_ps[:, m, :], prob_tiles[step][:, m * P : (m + 1) * P], identity[:])
-            f_ps_tiles[step] = f_ps
+                nc.tensor.transpose(views[m], prob_tiles[step][:, m * P : (m + 1) * P], identity[:])
+            f_ps_tiles[step] = views
 
         def weigh(step):
             c, s = divmod(step, S)
@@ -273,17 +292,19 @@ def tile_moe_pb_e_kernel(
                 sums = sums_tiles[c][:, m, :]
                 if s == 0:
                     nc.vector.tensor_scalar(
-                        out=sums, in0=f_ps_tiles[step][:, m, :], scalar1=weight, scalar2=None, op0=ALU.mult
+                        out=sums, in0=f_ps_tiles[step][m], scalar1=weight, scalar2=None, op0=ALU.mult
                     )
                 else:
                     nc.vector.scalar_tensor_tensor(
                         out=sums,
-                        in0=f_ps_tiles[step][:, m, :],
+                        in0=f_ps_tiles[step][m],
                         scalar=weight,
                         in1=sums,
                         op0=ALU.mult,
                         op1=ALU.add,
                     )
+                if step == STEPS - 1:
+                    nc.sync.dma_start(out=out_chunks[c][:, m, :], in_=sums)
 
         def chunk_due(step, lead):
             c, s = divmod(step + lead, S)
@@ -295,8 +316,10 @@ def tile_moe_pb_e_kernel(
                 enc_tiles[c] = load_chunk(c)
             if step < STEPS:
                 layer1(step)
-            if step + 2 < S:
-                sort_w1(step + 2)
+            if step + 1 < S:
+                sort_w1(step + 1)
+            if step == 0:
+                transpose_h0(1, 0)
             if 0 <= step - LAYER2_LAG < STEPS:
                 layer2(step - LAYER2_LAG)
             if 0 <= step - QUANTISE_LAG < STEPS:
@@ -307,7 +330,7 @@ def tile_moe_pb_e_kernel(
                 transpose_probs(step - TRANSPOSE_LAG)
             if 0 <= step - WEIGH_LAG < STEPS:
                 weigh(step - WEIGH_LAG)
-            if 0 <= step - STORE_LAG < STEPS and (step - STORE_LAG) % S == S - 1:
+            if 0 <= step - STORE_LAG < STEPS - 1 and (step - STORE_LAG) % S == S - 1:
                 c = (step - STORE_LAG) // S
                 nc.sync.dma_start(out=out_chunks[c], in_=sums_tiles[c][:])
             for half in range(2):
@@ -322,17 +345,15 @@ def tile_moe_pb_e_kernel(
                 quantise_h0(c)
 
         transpose_h0(0, 0)
-        widen_small_rows()
-        sort_w1_planes()
-        transpose_small_rows()
-        relu_h0(0, 0)
         transpose_h0(0, 1)
-        sort_w1(0)
-        keep_small_columns()
+        widen_small_rows()
+        relu_h0(0, 0)
         relu_h0(0, 1)
-        transpose_h0(1, 0)
+        transpose_small_rows()
+        sort_w1_planes()
+        sort_w1(0)
         quantise_h0(0)
-        sort_w1(1)
+        keep_small_columns()
 
         for step in range(STEPS + STORE_LAG):
             write_step(step)

@@ -27,7 +27,7 @@ STEPS = N_CHUNKS * S
 QUADRANTS = 4
 RUN = 4
 
-REGROUP_LAG = 2
+REGROUP_LAG = 3
 QUANTISE_LAG = REGROUP_LAG + 1
 LAYER2_LAG = QUANTISE_LAG + 1
 TRANSPOSE_LAG = LAYER2_LAG + 1

@@ -28,7 +28,7 @@ QUADRANTS = 4
 RUN = 4
 
 REGROUP_LAG = 3
-QUANTISE_LAG = REGROUP_LAG + 1
+QUANTISE_LAG = REGROUP_LAG
 LAYER2_LAG = QUANTISE_LAG + 1
 TRANSPOSE_LAG = LAYER2_LAG + 1
 WEIGH_LAG = TRANSPOSE_LAG + 1
@@ -283,11 +283,11 @@ def tile_moe_pb_e_kernel(
                 nc.tensor.transpose(views[m], prob_tiles[step][:, m * P : (m + 1) * P], identity[:])
             f_ps_tiles[step] = views
 
-        def weigh(step):
+        def weigh(step, tiles):
             c, s = divmod(step, S)
-            if s == 0:
+            if s == 0 and 0 in tiles:
                 sums_tiles[c] = sums_pool.tile([P, TILES, T], F32, name="sums")
-            for m in range(TILES):
+            for m in tiles:
                 weight = alpha_cols[:, s, c * TILES + m : c * TILES + m + 1]
                 sums = sums_tiles[c][:, m, :]
                 if s == 0:
@@ -322,14 +322,16 @@ def tile_moe_pb_e_kernel(
                 transpose_h0(1, 0)
             if 0 <= step - LAYER2_LAG < STEPS:
                 layer2(step - LAYER2_LAG)
-            if 0 <= step - QUANTISE_LAG < STEPS:
-                quantise_h1(step - QUANTISE_LAG)
             if 0 <= step - REGROUP_LAG < STEPS:
                 regroup_h1(step - REGROUP_LAG)
             if 0 <= step - TRANSPOSE_LAG < STEPS:
                 transpose_probs(step - TRANSPOSE_LAG)
             if 0 <= step - WEIGH_LAG < STEPS:
-                weigh(step - WEIGH_LAG)
+                weigh(step - WEIGH_LAG, range(0, HALF))
+            if 0 <= step - QUANTISE_LAG < STEPS:
+                quantise_h1(step - QUANTISE_LAG)
+            if 0 <= step - WEIGH_LAG < STEPS:
+                weigh(step - WEIGH_LAG, range(HALF, TILES))
             if 0 <= step - STORE_LAG < STEPS - 1 and (step - STORE_LAG) % S == S - 1:
                 c = (step - STORE_LAG) // S
                 nc.sync.dma_start(out=out_chunks[c], in_=sums_tiles[c][:])

@@ -38,6 +38,7 @@ H0_COPY_LEAD = (4, 2)
 H0_TRANSPOSE_LEAD = (5, 3)
 LOAD_LEAD = 3 * S
 HEAD_STEPS = 2
+SCALAR_WEIGH_STEP = STEPS - S
 
 FLOPS = 2 * S * N_TOKENS * H * (H + T)
 
@@ -231,42 +232,65 @@ def tile_moe_pb_e_kernel(
                 nc.sync.dma_start(out=sheets[tau:P:H_TILES, :, :], in_=y[:])
             sheets_tiles[step] = sheets
 
+        def token_pieces(step):
+            pieces = 2 if step == STEPS - 1 else 1
+            width = CHUNK // pieces
+            return [slice(i * width, (i + 1) * width) for i in range(pieces)]
+
         def regroup_h1(step):
             h1_grouped = h1_pool.tile([P, CHUNK * PACK], BF16, name="h1_grouped", align_bytes=64)
-            nc.vector.tensor_copy(
-                out=h1_grouped[:].rearrange("p (run r t) -> p run t r", r=RUN, t=PACK),
-                in_=sheets_tiles[step][:].rearrange("p t (run r) -> p run t r", r=RUN),
-            )
+            for tokens in token_pieces(step):
+                nc.vector.tensor_copy(
+                    out=h1_grouped[:, tokens.start * PACK : tokens.stop * PACK].rearrange(
+                        "p (run r t) -> p run t r", r=RUN, t=PACK
+                    ),
+                    in_=sheets_tiles[step][:, :, tokens].rearrange("p t (run r) -> p run t r", r=RUN),
+                )
             h1_grouped_tiles[step] = h1_grouped
 
         def quantise_h1(step):
             h1_codes = h1_pool.tile([P, CHUNK], I32, name="h1_codes", align_bytes=64)
             h1_plane = h1_pool.tile([P, CHUNK], U8, name="h1_plane", align_bytes=64)
-            nc.vector.quantize_mx(
-                out=h1_codes[:].bitcast(FP8X4), scales=h1_plane[:], in_=h1_grouped_tiles[step][:]
-            )
+            for tokens in token_pieces(step):
+                nc.vector.quantize_mx(
+                    out=h1_codes[:, tokens].bitcast(FP8X4),
+                    scales=h1_plane[:, tokens],
+                    in_=h1_grouped_tiles[step][:, tokens.start * PACK : tokens.stop * PACK],
+                )
             h1_operands[step] = (h1_codes, h1_plane)
 
         def layer2(step):
             s = step % S
             h1_codes, h1_plane = h1_operands[step]
-            z_ps = psum_z.tile([P, CHUNK], F32, name="z_ps")
-            nc.tensor.matmul_mx(
-                out=z_ps[:],
-                lhsT=w2_words[:, s, :].bitcast(FP8X4),
-                lhsT_scale=w2_planes[4 * s : P, :],
-                rhs=h1_codes[:].bitcast(FP8X4),
-                rhs_scale=h1_plane[:],
-                start=True,
-                stop=True,
-            )
+            z_views = {}
+            for tokens in token_pieces(step):
+                if step >= STEPS - S:
+                    z_ps = psum_x.tile([P, CHUNK], F32, name="x_ps")
+                else:
+                    z_ps = psum_z.tile([P, CHUNK], F32, name="z_ps")
+                width = tokens.stop - tokens.start
+                nc.tensor.matmul_mx(
+                    out=z_ps[:, 0:width],
+                    lhsT=w2_words[:, s, :].bitcast(FP8X4),
+                    lhsT_scale=w2_planes[4 * s : P, :],
+                    rhs=h1_codes[:, tokens].bitcast(FP8X4),
+                    rhs_scale=h1_plane[:, tokens],
+                    start=True,
+                    stop=True,
+                )
+                for first in range(tokens.start, tokens.stop, P):
+                    z_views[first] = z_ps[:, first - tokens.start : width]
             prob = prob_pool.tile([P, CHUNK], F32, name="prob")
             pieces = TILES if step == STEPS - 1 else 1
             width = CHUNK // pieces
             for i in range(pieces):
                 cols = slice(i * width, (i + 1) * width)
                 nc.scalar.activation(
-                    out=prob[:, cols], in_=z_ps[:, cols], func=ACT.Sigmoid, bias=b2_cols[:, s : s + 1], scale=1.0
+                    out=prob[:, cols],
+                    in_=z_views[cols.start][:, 0:width],
+                    func=ACT.Sigmoid,
+                    bias=b2_cols[:, s : s + 1],
+                    scale=1.0,
                 )
             prob_tiles[step] = prob
 
@@ -290,7 +314,9 @@ def tile_moe_pb_e_kernel(
             for m in tiles:
                 weight = alpha_cols[:, s, c * TILES + m : c * TILES + m + 1]
                 sums = sums_tiles[c][:, m, :]
-                if s == 0:
+                if step == SCALAR_WEIGH_STEP:
+                    nc.scalar.activation(out=sums, in_=f_ps_tiles[step][m], func=ACT.Copy, scale=weight)
+                elif s == 0:
                     nc.vector.tensor_scalar(
                         out=sums, in0=f_ps_tiles[step][m], scalar1=weight, scalar2=None, op0=ALU.mult
                     )
@@ -326,12 +352,16 @@ def tile_moe_pb_e_kernel(
                 regroup_h1(step - REGROUP_LAG)
             if 0 <= step - TRANSPOSE_LAG < STEPS:
                 transpose_probs(step - TRANSPOSE_LAG)
-            if 0 <= step - WEIGH_LAG < STEPS:
-                weigh(step - WEIGH_LAG, range(0, HALF))
+            between = HALF if step - QUANTISE_LAG < STEPS - 1 else 0
+            if step - TRANSPOSE_LAG == SCALAR_WEIGH_STEP:
+                weigh(SCALAR_WEIGH_STEP, range(TILES))
+            vector_weighs = 0 <= step - WEIGH_LAG < STEPS and step - WEIGH_LAG != SCALAR_WEIGH_STEP
+            if vector_weighs:
+                weigh(step - WEIGH_LAG, range(0, between))
             if 0 <= step - QUANTISE_LAG < STEPS:
                 quantise_h1(step - QUANTISE_LAG)
-            if 0 <= step - WEIGH_LAG < STEPS:
-                weigh(step - WEIGH_LAG, range(HALF, TILES))
+            if vector_weighs:
+                weigh(step - WEIGH_LAG, range(between, TILES))
             if 0 <= step - STORE_LAG < STEPS - 1 and (step - STORE_LAG) % S == S - 1:
                 c = (step - STORE_LAG) // S
                 nc.sync.dma_start(out=out_chunks[c], in_=sums_tiles[c][:])

@@ -37,7 +37,7 @@ H0_QUANTISE_LEAD = 1
 H0_COPY_LEAD = (4, 2)
 H0_TRANSPOSE_LEAD = (5, 3)
 LOAD_LEAD = 3 * S
-HEAD_STEPS = 2
+HEAD_STEPS = 0
 SCALAR_WEIGH_STEP = STEPS - S
 
 FLOPS = 2 * S * N_TOKENS * H * (H + T)

@@ -55,7 +55,7 @@ def tile_moe_pb_e_kernel(
         const = ctx.enter_context(tc.tile_pool(name="const", bufs=1))
         enc_pool = ctx.enter_context(tc.tile_pool(name="enc", bufs=4))
         h0_pool = ctx.enter_context(tc.tile_pool(name="h0", bufs=2))
-        y_pool = ctx.enter_context(tc.tile_pool(name="y", bufs=2 * H_TILES))
+        y_pool = ctx.enter_context(tc.tile_pool(name="y", bufs=3))
         sheets_pool = ctx.enter_context(tc.tile_pool(name="sheets", bufs=REGROUP_LAG + 2))
         h1_pool = ctx.enter_context(tc.tile_pool(name="h1", bufs=3))
         prob_pool = ctx.enter_context(tc.tile_pool(name="prob", bufs=3))
@@ -221,15 +221,17 @@ def tile_moe_pb_e_kernel(
                     start=True,
                     stop=True,
                 )
-                y = y_pool.tile([P, CHUNK], BF16, name="y")
+                if tau == 0:
+                    y_step = y_pool.tile([P, H_TILES, CHUNK], BF16, name="y")
+                y = y_step[:, tau, :]
                 bias = b1_cols[:, tau, s : s + 1]
                 if step < HEAD_STEPS and tau % 2 == 1:
                     nc.vector.tensor_scalar(
-                        out=y[:], in0=x_ps[:], scalar1=bias, scalar2=0.0, op0=ALU.add, op1=ALU.max
+                        out=y, in0=x_ps[:], scalar1=bias, scalar2=0.0, op0=ALU.add, op1=ALU.max
                     )
                 else:
-                    nc.scalar.activation(out=y[:], in_=x_ps[:], func=ACT.Relu, bias=bias, scale=1.0)
-                nc.sync.dma_start(out=sheets[tau:P:H_TILES, :, :], in_=y[:])
+                    nc.scalar.activation(out=y, in_=x_ps[:], func=ACT.Relu, bias=bias, scale=1.0)
+                nc.sync.dma_start(out=sheets[tau:P:H_TILES, :, :], in_=y)
             sheets_tiles[step] = sheets
 
         def token_pieces(step):

from contextlib import ExitStack

import concourse.mybir as mybir
from concourse.masks import make_identity

F32 = mybir.dt.float32
BF16 = mybir.dt.bfloat16
I32 = mybir.dt.int32
U8 = mybir.dt.uint8
FP8X4 = mybir.dt.float8_e4m3fn_x4
ACT = mybir.ActivationFunctionType
ALU = mybir.AluOpType

P = 128
PACK = 4
N_TOKENS = 4096
H = 512
S = 4
T = 128
CHUNK = 512
TILES = CHUNK // P
HALF = TILES // 2
N_CHUNKS = N_TOKENS // CHUNK
N_TILES = N_TOKENS // P
H_TILES = H // P
STEPS = N_CHUNKS * S
QUADRANTS = 4
RUN = 4

REGROUP_LAG = 3
QUANTISE_LAG = REGROUP_LAG
LAYER2_LAG = QUANTISE_LAG + 1
TRANSPOSE_LAG = LAYER2_LAG + 1
WEIGH_LAG = TRANSPOSE_LAG + 1
STORE_LAG = WEIGH_LAG + 1
H0_QUANTISE_LEAD = 1
H0_COPY_LEAD = (4, 2)
H0_TRANSPOSE_LEAD = (5, 3)
LOAD_LEAD = 3 * S
HEAD_STEPS = 0
SCALAR_WEIGH_STEP = STEPS - S

FLOPS = 2 * S * N_TOKENS * H * (H + T)


def tile_moe_pb_e_kernel(
    tc, encodings, alphas, W1_words, W1_scales, b1, W2_words, W2_scales, b2, out
):
    nc = tc.nc
    enc_chunks = encodings.rearrange("(c m p) h -> c p m h", m=TILES, p=P)
    out_chunks = out.rearrange("(c m p) o -> c p m o", m=TILES, p=P)

    with ExitStack() as ctx:
        ctx.enter_context(tc.manual_schedule())
        const = ctx.enter_context(tc.tile_pool(name="const", bufs=1))
        enc_pool = ctx.enter_context(tc.tile_pool(name="enc", bufs=4))
        h0_pool = ctx.enter_context(tc.tile_pool(name="h0", bufs=2))
        y_pool = ctx.enter_context(tc.tile_pool(name="y", bufs=3))
        sheets_pool = ctx.enter_context(tc.tile_pool(name="sheets", bufs=REGROUP_LAG + 2))
        h1_pool = ctx.enter_context(tc.tile_pool(name="h1", bufs=3))
        prob_pool = ctx.enter_context(tc.tile_pool(name="prob", bufs=3))
        sums_pool = ctx.enter_context(tc.tile_pool(name="sums", bufs=2))
        psum_x = ctx.enter_context(tc.psum_pool(name="psum_x", bufs=4))
        psum_e = ctx.enter_context(tc.psum_pool(name="psum_e", bufs=1))
        psum_z = ctx.enter_context(tc.psum_pool(name="psum_z", bufs=1))
        psum_f = ctx.enter_context(tc.psum_pool(name="psum_f", bufs=2))

        def load_chunk(c):
            enc_sb = enc_pool.tile([P, TILES, H], BF16, name="enc_sb")
            if c == 0:
                for m in range(TILES):
                    nc.sync.dma_start(out=enc_sb[:, m, :], in_=enc_chunks[c][:, m, :])
            else:
                nc.sync.dma_start(out=enc_sb[:], in_=enc_chunks[c])
            return enc_sb

        bias_rows = const.tile([P, H + T], BF16, name="bias_rows")
        nc.vector.memset(bias_rows[:], 0.0)
        alpha_rows = const.tile([P, P], BF16, name="alpha_rows")
        w1_planes_in = const.tile([P, H], U8, name="w1_planes_in", align_bytes=64)
        w2_planes = const.tile([P, T], U8, name="w2_planes", align_bytes=64)
        nc.vector.memset(w1_planes_in[:].bitcast(I32), 0)
        nc.vector.memset(w2_planes[:].bitcast(I32), 0)
        identity = const.tile([P, P], F32, name="identity")
        make_identity(nc, identity[:])
        warm = const.tile([P, 2], F32, name="warm")
        nc.gpsimd.memset(warm[:, 0:1], 0.0)
        nc.scalar.activation(out=warm[:, 1:2], in_=warm[:, 0:1], func=ACT.Sigmoid)

        def load_planes(planes, scales):
            for quadrant in range(QUADRANTS):
                nc.sync.dma_start(
                    out=planes[32 * quadrant : 32 * quadrant + 4 * S, :].bitcast(I32),
                    in_=scales[:, 4 * quadrant : 4 * quadrant + 4, :].bitcast(I32),
                )

        w1_in = const.tile([P, S, H], I32, name="w1_in", align_bytes=64)

        def load_w1(s):
            nc.sync.dma_start(
                out=w1_in[:, s, :], in_=W1_words[s].rearrange("p col t -> p (col t)").bitcast(I32)
            )

        enc_tiles = {0: load_chunk(0)}
        nc.sync.dma_start(out=bias_rows[0:S, 0:H], in_=b1)
        nc.sync.dma_start(out=bias_rows[0:S, H : H + T], in_=b2)
        nc.sync.dma_start(out=alpha_rows[:], in_=alphas.rearrange("s (j p) -> (s j) p", p=P))
        load_planes(w1_planes_in, W1_scales)
        load_w1(0)
        load_w1(1)
        enc_tiles[1] = load_chunk(1)
        for s in range(2, S):
            load_w1(s)
        load_planes(w2_planes, W2_scales)
        w2_words = const.tile([P, S, T], I32, name="w2_words", align_bytes=64)
        nc.sync.dma_start(
            out=w2_words[:], in_=W2_words.rearrange("s p col t -> p s (col t)").bitcast(I32)
        )
        enc_tiles[2] = load_chunk(2)

        w1_planes = const.tile([P, H_TILES, P], U8, name="w1_planes", align_bytes=64)
        w1_tiles = const.tile([P, S, H_TILES, P], I32, name="w1_tiles", align_bytes=64)

        def sort_w1_planes():
            nc.vector.tensor_copy(
                out=w1_planes[:].bitcast(I32),
                in_=w1_planes_in[:].bitcast(I32).rearrange("p (a tau) -> p tau a", tau=H_TILES),
            )

        def sort_w1(s):
            nc.vector.tensor_copy(
                out=w1_tiles[:, s, :, :].rearrange("p tau (a i) -> p tau a i", i=PACK),
                in_=w1_in[:, s, :].rearrange("p (a tau i) -> p tau a i", tau=H_TILES, i=PACK),
            )

        strips = H_TILES + 2
        small_rows = const.tile([P, strips, P], F32, name="small_rows")
        b1_cols = const.tile([P, H_TILES, S], F32, name="b1_cols")
        b2_cols = const.tile([P, S], F32, name="b2_cols")
        alpha_cols = const.tile([P, S, N_TILES], F32, name="alpha_cols")
        small_ps = {}

        def widen_small_rows():
            nc.scalar.copy(
                out=small_rows[:, 0:H_TILES, :].rearrange("p tau (a i) -> p tau a i", i=PACK),
                in_=bias_rows[:, 0:H].rearrange("p (a tau i) -> p tau a i", tau=H_TILES, i=PACK),
            )
            nc.scalar.copy(out=small_rows[:, H_TILES, :], in_=bias_rows[:, H : H + T])
            nc.scalar.copy(out=small_rows[:, H_TILES + 1, :], in_=alpha_rows[:])

        def transpose_small_rows():
            for bank in range(2):
                small_ps[bank] = psum_f.tile([P, H_TILES, P], F32, name="f_ps")
            for strip in range(strips):
                bank, place = divmod(strip, H_TILES)
                nc.tensor.transpose(small_ps[bank][:, place, :], small_rows[:, strip, :], identity[:])

        def keep_small_columns():
            nc.scalar.copy(out=b1_cols[:], in_=small_ps[0][:, :, 0:S])
            nc.scalar.copy(out=b2_cols[:], in_=small_ps[1][:, 0, 0:S])
            nc.scalar.copy(out=alpha_cols[:].rearrange("p s j -> p (s j)"), in_=small_ps[1][:, 1, :])

        h0_grouped_tiles = {}
        e_ps_tiles = {}
        h0_operands = {}
        sheets_tiles = {}
        h1_grouped_tiles = {}
        h1_operands = {}
        prob_tiles = {}
        f_ps_tiles = {}
        sums_tiles = {}

        def transpose_h0(c, half):
            if c == 0 and half == 1:
                x_ps = psum_x.tile([P, CHUNK], F32, name="x_ps")
                e_ps = x_ps[:].rearrange("p (m u n) -> p m u n", m=HALF, u=2)
            else:
                e_tile = psum_e.tile([P, HALF, 2, P], F32, name="e_ps")
                e_ps = e_tile[:]
            for m in range(HALF):
                pairs = enc_tiles[c][:, HALF * half + m, :].bitcast(F32)
                for u in range(2):
                    nc.tensor.transpose(e_ps[:, m, u, :], pairs[:, u : H // 2 : 2], identity[:])
            e_ps_tiles[c, half] = e_ps

        def relu_h0(c, half):
            if half == 0:
                h0_grouped_tiles[c] = h0_pool.tile(
                    [P, CHUNK * PACK], BF16, name="h0_grouped", align_bytes=64
                )
            grouped = h0_grouped_tiles[c][:].rearrange("p (m n u e) -> p m n u e", m=TILES, u=2, e=2)
            for m in range(HALF):
                nc.vector.tensor_scalar_max(
                    out=grouped[:, HALF * half + m, :, :, :],
                    in0=e_ps_tiles[c, half][:, m, :, :]
                    .bitcast(BF16)
                    .rearrange("p u (n e) -> p n u e", e=2),
                    scalar1=0.0,
                )

        def quantise_h0(c):
            h0_codes = h0_pool.tile([P, CHUNK], I32, name="h0_codes", align_bytes=64)
            h0_plane = h0_pool.tile([P, CHUNK], U8, name="h0_plane", align_bytes=64)
            nc.vector.quantize_mx(
                out=h0_codes[:].bitcast(FP8X4), scales=h0_plane[:], in_=h0_grouped_tiles[c][:]
            )
            h0_operands[c] = (h0_codes, h0_plane)

        def layer1(step):
            c, s = divmod(step, S)
            h0_codes, h0_plane = h0_operands[c]
            sheets = sheets_pool.tile([P, PACK, CHUNK], BF16, name="sheets")
            for tau in range(H_TILES):
                x_ps = psum_x.tile([P, CHUNK], F32, name="x_ps")
                nc.tensor.matmul_mx(
                    out=x_ps[:],
                    lhsT=w1_tiles[:, s, tau, :].bitcast(FP8X4),
                    lhsT_scale=w1_planes[4 * s : P, tau, :],
                    rhs=h0_codes[:].bitcast(FP8X4),
                    rhs_scale=h0_plane[:],
                    start=True,
                    stop=True,
                )
                if tau == 0:
                    y_step = y_pool.tile([P, H_TILES, CHUNK], BF16, name="y")
                y = y_step[:, tau, :]
                bias = b1_cols[:, tau, s : s + 1]
                if step < HEAD_STEPS and tau % 2 == 1:
                    nc.vector.tensor_scalar(
                        out=y, in0=x_ps[:], scalar1=bias, scalar2=0.0, op0=ALU.add, op1=ALU.max
                    )
                else:
                    nc.scalar.activation(out=y, in_=x_ps[:], func=ACT.Relu, bias=bias, scale=1.0)
                nc.sync.dma_start(out=sheets[tau:P:H_TILES, :, :], in_=y)
            sheets_tiles[step] = sheets

        def token_pieces(step):
            pieces = 2 if step == STEPS - 1 else 1
            width = CHUNK // pieces
            return [slice(i * width, (i + 1) * width) for i in range(pieces)]

        def regroup_h1(step):
            h1_grouped = h1_pool.tile([P, CHUNK * PACK], BF16, name="h1_grouped", align_bytes=64)
            for tokens in token_pieces(step):
                nc.vector.tensor_copy(
                    out=h1_grouped[:, tokens.start * PACK : tokens.stop * PACK].rearrange(
                        "p (run r t) -> p run t r", r=RUN, t=PACK
                    ),
                    in_=sheets_tiles[step][:, :, tokens].rearrange("p t (run r) -> p run t r", r=RUN),
                )
            h1_grouped_tiles[step] = h1_grouped

        def quantise_h1(step):
            h1_codes = h1_pool.tile([P, CHUNK], I32, name="h1_codes", align_bytes=64)
            h1_plane = h1_pool.tile([P, CHUNK], U8, name="h1_plane", align_bytes=64)
            for tokens in token_pieces(step):
                nc.vector.quantize_mx(
                    out=h1_codes[:, tokens].bitcast(FP8X4),
                    scales=h1_plane[:, tokens],
                    in_=h1_grouped_tiles[step][:, tokens.start * PACK : tokens.stop * PACK],
                )
            h1_operands[step] = (h1_codes, h1_plane)

        def layer2(step):
            s = step % S
            h1_codes, h1_plane = h1_operands[step]
            z_views = {}
            for tokens in token_pieces(step):
                if step >= STEPS - S:
                    z_ps = psum_x.tile([P, CHUNK], F32, name="x_ps")
                else:
                    z_ps = psum_z.tile([P, CHUNK], F32, name="z_ps")
                width = tokens.stop - tokens.start
                nc.tensor.matmul_mx(
                    out=z_ps[:, 0:width],
                    lhsT=w2_words[:, s, :].bitcast(FP8X4),
                    lhsT_scale=w2_planes[4 * s : P, :],
                    rhs=h1_codes[:, tokens].bitcast(FP8X4),
                    rhs_scale=h1_plane[:, tokens],
                    start=True,
                    stop=True,
                )
                for first in range(tokens.start, tokens.stop, P):
                    z_views[first] = z_ps[:, first - tokens.start : width]
            prob = prob_pool.tile([P, CHUNK], F32, name="prob")
            pieces = TILES if step == STEPS - 1 else 1
            width = CHUNK // pieces
            for i in range(pieces):
                cols = slice(i * width, (i + 1) * width)
                nc.scalar.activation(
                    out=prob[:, cols],
                    in_=z_views[cols.start][:, 0:width],
                    func=ACT.Sigmoid,
                    bias=b2_cols[:, s : s + 1],
                    scale=1.0,
                )
            prob_tiles[step] = prob

        def transpose_probs(step):
            if step == STEPS - 1:
                views = []
                for m in range(TILES):
                    x_ps = psum_x.tile([P, CHUNK], F32, name="x_ps")
                    views.append(x_ps[:, 0:T])
            else:
                f_ps = psum_f.tile([P, TILES, T], F32, name="f_ps")
                views = [f_ps[:, m, :] for m in range(TILES)]
            for m in range(TILES):
                nc.tensor.transpose(views[m], prob_tiles[step][:, m * P : (m + 1) * P], identity[:])
            f_ps_tiles[step] = views

        def weigh(step, tiles):
            c, s = divmod(step, S)
            if s == 0 and 0 in tiles:
                sums_tiles[c] = sums_pool.tile([P, TILES, T], F32, name="sums")
            for m in tiles:
                weight = alpha_cols[:, s, c * TILES + m : c * TILES + m + 1]
                sums = sums_tiles[c][:, m, :]
                if step == SCALAR_WEIGH_STEP:
                    nc.scalar.activation(out=sums, in_=f_ps_tiles[step][m], func=ACT.Copy, scale=weight)
                elif s == 0:
                    nc.vector.tensor_scalar(
                        out=sums, in0=f_ps_tiles[step][m], scalar1=weight, scalar2=None, op0=ALU.mult
                    )
                else:
                    nc.vector.scalar_tensor_tensor(
                        out=sums,
                        in0=f_ps_tiles[step][m],
                        scalar=weight,
                        in1=sums,
                        op0=ALU.mult,
                        op1=ALU.add,
                    )
                if step == STEPS - 1:
                    nc.sync.dma_start(out=out_chunks[c][:, m, :], in_=sums)

        def chunk_due(step, lead):
            c, s = divmod(step + lead, S)
            return c if s == 0 and 0 <= c < N_CHUNKS else None

        def write_step(step):
            c = chunk_due(step, LOAD_LEAD)
            if c is not None:
                enc_tiles[c] = load_chunk(c)
            if step < STEPS:
                layer1(step)
            if step + 1 < S:
                sort_w1(step + 1)
            if step == 0:
                transpose_h0(1, 0)
            if 0 <= step - LAYER2_LAG < STEPS:
                layer2(step - LAYER2_LAG)
            if 0 <= step - REGROUP_LAG < STEPS:
                regroup_h1(step - REGROUP_LAG)
            if 0 <= step - TRANSPOSE_LAG < STEPS:
                transpose_probs(step - TRANSPOSE_LAG)
            between = HALF if step - QUANTISE_LAG < STEPS - 1 else 0
            if step - TRANSPOSE_LAG == SCALAR_WEIGH_STEP:
                weigh(SCALAR_WEIGH_STEP, range(TILES))
            vector_weighs = 0 <= step - WEIGH_LAG < STEPS and step - WEIGH_LAG != SCALAR_WEIGH_STEP
            if vector_weighs:
                weigh(step - WEIGH_LAG, range(0, between))
            if 0 <= step - QUANTISE_LAG < STEPS:
                quantise_h1(step - QUANTISE_LAG)
            if vector_weighs:
                weigh(step - WEIGH_LAG, range(between, TILES))
            if 0 <= step - STORE_LAG < STEPS - 1 and (step - STORE_LAG) % S == S - 1:
                c = (step - STORE_LAG) // S
                nc.sync.dma_start(out=out_chunks[c], in_=sums_tiles[c][:])
            for half in range(2):
                c = chunk_due(step, H0_TRANSPOSE_LEAD[half])
                if c is not None:
                    transpose_h0(c, half)
                c = chunk_due(step, H0_COPY_LEAD[half])
                if c is not None:
                    relu_h0(c, half)
            c = chunk_due(step, H0_QUANTISE_LEAD)
            if c is not None:
                quantise_h0(c)

        transpose_h0(0, 0)
        transpose_h0(0, 1)
        widen_small_rows()
        relu_h0(0, 0)
        relu_h0(0, 1)
        transpose_small_rows()
        sort_w1_planes()
        sort_w1(0)
        quantise_h0(0)
        keep_small_columns()

        for step in range(STEPS + STORE_LAG):
            write_step(step)
